import numpy as np
import ml_dtypes


def mxq(x, axis, fmt="e4m3"):
    dtype, down = {"e4m3": (ml_dtypes.float8_e4m3fn, 7), "e5m2": (ml_dtypes.float8_e5m2, 14)}[fmt]
    v = np.moveaxis(np.asarray(x, np.float32).astype(ml_dtypes.bfloat16).astype(np.float64), axis, -1)
    blocks = v.reshape(v.shape[:-1] + (-1, 32))
    amax = np.abs(blocks).max(-1, keepdims=True)
    byte = np.maximum(np.where(amax > 0, np.frexp(amax)[1] - 1 + 127, 0) - down, 1)
    scale = np.exp2(byte - 127.0)
    codes = (blocks / scale).astype(np.float32).astype(dtype).astype(np.float64)
    return np.moveaxis((codes * scale).reshape(v.shape), -1, axis)


WIDE = False


def mx_kscale(k):
    if not WIDE:
        return np.ones(k)
    levels = np.array([30, -30])
    if k % 512:
        return np.exp2(np.random.permutation(np.resize(levels, k // 32))).repeat(32)
    a = np.empty((k // 512, 16))
    for p in range(k // 512):
        a[p, :8] = np.random.permutation(np.resize(levels, 8))
        for g in range(8):
            far = levels[np.abs(levels - a[p, g]) >= 10]
            a[p, g + 8] = far[np.random.randint(len(far))]
    return np.exp2(a.ravel()).repeat(32)


BF16 = ml_dtypes.bfloat16


def bf(x):
    return np.asarray(x, np.float32).astype(BF16)


def f64(x):
    return np.asarray(x).astype(np.float64)


B, S, HID, H, KV, D = 1, 512, 2048, 16, 4, 128
EPS = 1e-6
THETA = 10000.0
HALF = D // 2


def rotate_half(x):
    return np.concatenate([-x[..., HALF:], x[..., :HALF]], axis=-1)


def rms_norm(x, w=None):
    n = x * (1.0 / np.sqrt(np.mean(x * x, axis=-1, keepdims=True) + EPS))
    return n if w is None else n * w


def setup_inputs():
    s = mx_kscale(HID)
    c = 0.004 / np.sqrt(HID)
    inv_freq = 1.0 / THETA ** (np.arange(0, D, 2) / D)
    pos = np.random.randint(0, S) + np.arange(S)
    freqs = pos[:, None] * inv_freq[None, :]
    emb = np.concatenate([freqs, freqs], axis=-1)
    return {"hidden_states": bf(np.random.standard_normal((B, S, HID)) * s),
            "cos": bf(np.cos(emb)[None]),
            "sin": bf(np.sin(emb)[None]),
            "Wq": bf(np.random.standard_normal((H * D, HID)) * c / s[None, :]),
            "Wk": bf(np.random.standard_normal((KV * D, HID)) * c / s[None, :]),
            "Wv": bf(np.random.standard_normal((KV * D, HID)) * c / s[None, :]),
            "q_norm_w": bf(0.5 + 0.1 * np.random.standard_normal(D)),
            "k_norm_w": bf(0.5 + 0.1 * np.random.standard_normal(D))}


def reference(hidden_states, cos, sin, Wq, Wk, Wv, q_norm_w, k_norm_w):
    xq = mxq(f64(hidden_states), 2, "e5m2")
    cs = f64(cos)[:, :, None, :]
    sn = f64(sin)[:, :, None, :]
    q = (xq @ mxq(f64(Wq).T, 0, "e5m2")).reshape(B, S, H, D)
    k = (xq @ mxq(f64(Wk).T, 0, "e5m2")).reshape(B, S, KV, D)
    v = (xq @ mxq(f64(Wv).T, 0, "e5m2")).reshape(B, S, KV, D)
    q = rms_norm(q, f64(q_norm_w))
    q = q * cs + rotate_half(q) * sn
    k = rms_norm(k, f64(k_norm_w))
    k = k * cs + rotate_half(k) * sn
    v = rms_norm(v)
    return q.transpose(0, 2, 1, 3), k.transpose(0, 2, 1, 3), v.transpose(0, 2, 1, 3)

@@ -1,0 +1,242 @@
+from contextlib import ExitStack
+
+import concourse.mybir as mybir
+from concourse.masks import make_identity
+
+S, HID, H, KV, D = 512, 2048, 16, 4, 128
+EPS = 1e-6
+HALF = D // 2
+FLOPS = 2 * S * HID * (H + 2 * KV) * D
+
+F32 = mybir.dt.float32
+BF16 = mybir.dt.bfloat16
+U32 = mybir.dt.uint32
+U8 = mybir.dt.uint8
+E5M2X4 = mybir.dt.float8_e5m2_x4
+ACT = mybir.ActivationFunctionType
+ALU = mybir.AluOpType
+
+P = 128
+K_PASS = 512
+PASSES = HID // K_PASS
+TOKEN_TILES = S // P
+HEADS = 4
+GROUPS = (H + 2 * KV) // HEADS
+K_GROUP = H // HEADS
+V_GROUP = K_GROUP + 1
+WORDS = K_PASS // 2
+STEPS = GROUPS * TOKEN_TILES
+
+
+def tile_refattention_pa_kernel(
+    tc, hidden_states, cos, sin, Wq, Wk, Wv, q_norm_w, k_norm_w, out_0, out_1, out_2
+):
+    nc = tc.nc
+    weights = [Wq[g * HEADS * D : (g + 1) * HEADS * D, :] for g in range(K_GROUP)] + [Wk, Wv]
+    outs = [out_0[0, g * HEADS : (g + 1) * HEADS] for g in range(K_GROUP)] + [out_1[0], out_2[0]]
+
+    with ExitStack() as ctx:
+        keep = ctx.enter_context(tc.tile_pool(name="keep", bufs=1))
+        ring = ctx.enter_context(tc.tile_pool(name="ring", bufs=3))
+        psum = ctx.enter_context(tc.psum_pool(name="psum", bufs=4))
+        ctx.enter_context(tc.manual_schedule())
+
+        gains = []
+        for name, gain in (("q_gain", q_norm_w), ("k_gain", k_norm_w)):
+            spread = keep.tile([P, 1, D], BF16, name=name)
+            nc.scalar.dma_start(out=spread[:, 0, :], in_=gain.partition_broadcast(P))
+            gains.append(spread)
+
+        ident = keep.tile([P, P], F32)
+        make_identity(nc, ident[:])
+
+        blocks = {}
+        x_rows = hidden_states[0].rearrange("(p j) k -> p j k", j=TOKEN_TILES)
+
+        def load_x(j):
+            raw = keep.tile([P, HID], BF16, name="x_raw%d" % j)
+            nc.sync.dma_start(out=raw[:], in_=x_rows[:, j, :])
+            words = raw[:].bitcast(F32)
+            blocks[("x", j)] = [words[:, c * WORDS : (c + 1) * WORDS] for c in range(PASSES)]
+
+        def load_w(g, c0, n):
+            raw = keep.tile([P, HEADS, n * K_PASS], BF16, name="w_raw%d_%d" % (g, c0))
+            rows = weights[g].rearrange("(h p) k -> p h k", p=P)
+            nc.sync.dma_start(out=raw[:], in_=rows[:, :, c0 * K_PASS : (c0 + n) * K_PASS])
+            for c in range(n):
+                blocks[("w", g, c0 + c)] = [
+                    raw[:, h, :].bitcast(F32)[:, c * WORDS : (c + 1) * WORDS] for h in range(HEADS)
+                ]
+
+        cos_sb = keep.tile([P, TOKEN_TILES, D], BF16)
+        sin_sb = keep.tile([P, TOKEN_TILES, D], BF16)
+        load_w(0, 0, 1)
+        load_x(0)
+        for c in range(1, PASSES):
+            load_w(0, c, 1)
+        load_x(1)
+        nc.sync.dma_start(out=cos_sb[:], in_=cos[0].rearrange("(p j) d -> p j d", j=TOKEN_TILES))
+        nc.sync.dma_start(out=sin_sb[:], in_=sin[0].rearrange("(p j) d -> p j d", j=TOKEN_TILES))
+        load_w(1, 0, 1)
+        load_x(2)
+        load_w(1, 1, 1)
+        load_x(3)
+        load_w(1, 2, 2)
+        for g in range(2, GROUPS):
+            load_w(g, 0, 2)
+            load_w(g, 2, 2)
+
+        units = [("w", 0, 0), ("x", 0), ("w", 0, 1), ("w", 0, 2), ("w", 0, 3), ("x", 1)]
+        units += [("w", 1, 0), ("x", 2), ("w", 1, 1), ("x", 3), ("w", 1, 2), ("w", 1, 3)]
+        units += [("w", g, c) for g in range(2, GROUPS) for c in range(PASSES)]
+
+        banks, grouped, quantised = {}, {}, {}
+
+        def transpose(unit):
+            banks[unit] = []
+            for half in range(2):
+                bank = psum.tile([P, 2, 2, P], F32, name="turned")
+                for a in range(2):
+                    for u in range(2):
+                        nc.tensor.transpose(bank[:, a, u, :], blocks[unit][2 * half + a][:, u:WORDS:2], ident[:])
+                banks[unit].append(bank)
+            staged = ring.tile([P, 4 * K_PASS], BF16, name="grouped", align_bytes=64)
+            grouped[unit] = staged
+
+        def empty(unit, half):
+            words = grouped[unit][:].bitcast(F32)[:, half * 2 * WORDS : (half + 1) * 2 * WORDS]
+            nc.scalar.copy(
+                out=words.rearrange("p (a r u) -> p a r u", a=2, u=2),
+                in_=banks[unit][half][:].rearrange("p a u r -> p a r u"),
+            )
+
+        def quantise(unit):
+            kind, bufs = ("x", TOKEN_TILES) if unit[0] == "x" else ("w", 2 * PASSES)
+            codes = ring.tile([P, K_PASS], U32, name=kind + "_codes", bufs=bufs, align_bytes=64)
+            scales = ring.tile([P, K_PASS], U8, name=kind + "_scales", bufs=bufs, align_bytes=64)
+            nc.vector.quantize_mx(out=codes[:].bitcast(E5M2X4), scales=scales[:], in_=grouped[unit][:])
+            quantised[unit] = (codes, scales)
+
+        tables = []
+
+        def make_table(gain):
+            table = keep.tile([P, TOKEN_TILES, 2, D], F32, name="table%d" % len(tables))
+            nc.vector.tensor_tensor(
+                out=table[:, :, 0, :], in0=cos_sb[:], in1=gain[:].to_broadcast([P, TOKEN_TILES, D]), op=ALU.mult
+            )
+            nc.vector.tensor_tensor(
+                out=table[:, :, 1, :HALF],
+                in0=sin_sb[:, :, HALF:],
+                in1=gain[:, :, :HALF].to_broadcast([P, TOKEN_TILES, HALF]),
+                op=ALU.mult,
+            )
+            nc.vector.scalar_tensor_tensor(
+                out=table[:, :, 1, HALF:],
+                in0=sin_sb[:, :, :HALF],
+                scalar=-1.0,
+                in1=gain[:, :, HALF:].to_broadcast([P, TOKEN_TILES, HALF]),
+                op0=ALU.mult,
+                op1=ALU.mult,
+            )
+            tables.append(table)
+
+        def multiply(g, j):
+            acc = psum.tile([P, HEADS, D], F32, name="acc")
+            x_codes, x_scales = quantised[("x", j)]
+            for c in range(PASSES):
+                w_codes, w_scales = quantised[("w", g, c)]
+                nc.tensor.matmul_mx(
+                    out=acc[:].rearrange("p h d -> p (h d)"),
+                    lhsT=x_codes[:, c * P : (c + 1) * P].bitcast(E5M2X4),
+                    lhsT_scale=x_scales[:, c * P : (c + 1) * P],
+                    rhs=w_codes[:].bitcast(E5M2X4),
+                    rhs_scale=w_scales[:],
+                    start=(c == 0),
+                    stop=(c == PASSES - 1),
+                )
+            return acc
+
+        def sum_squares(acc):
+            sums = ring.tile([P, HEADS], F32, name="sums")
+            squares = ring.tile([P, HEADS, D], F32, name="squares", bufs=2)
+            for h in range(HEADS):
+                nc.scalar.activation(
+                    out=squares[:, h, :], in_=acc[:, h, :], func=ACT.Square, accum_out=sums[:, h : h + 1]
+                )
+            return sums
+
+        def inverse_rms(sums):
+            inv = ring.tile([P, HEADS, 1], F32, name="inv")
+            nc.scalar.activation(out=inv[:, :, 0], in_=sums[:], func=ACT.Abs_reciprocal_sqrt, scale=1.0 / D, bias=EPS)
+            return inv
+
+        def products(acc, inv, table, j):
+            terms = ring.tile([P, HEADS, 2, D], F32, name="terms", bufs=2)
+            for h in range(HEADS):
+                nc.vector.scalar_tensor_tensor(
+                    out=terms[:, h, :, :],
+                    in0=acc[:, h : h + 1, :].to_broadcast([P, 2, D]),
+                    scalar=inv[:, h, :],
+                    in1=table[:, j, :, :],
+                    op0=ALU.mult,
+                    op1=ALU.mult,
+                )
+            return terms
+
+        def add_terms(terms, result, j):
+            nc.vector.tensor_tensor(
+                out=result[:, :, j, :].rearrange("p h (t i) -> p h t i", t=2),
+                in0=terms[:, :, 0, :].rearrange("p h (t i) -> p h t i", t=2),
+                in1=terms[:, :, 1, :].rearrange("p h (t i) -> p h t i", t=2)[:, :, ::-1, :],
+                op=ALU.add,
+            )
+
+        def store(g, result, j0, j1):
+            dest = outs[g].rearrange("h (p j) d -> p h (j d)", j=TOKEN_TILES)
+            nc.sync.dma_start(
+                out=dest[:, :, j0 * D : j1 * D],
+                in_=result[:].rearrange("p h j d -> p h (j d)")[:, :, j0 * D : j1 * D],
+            )
+
+        first = PASSES + 2
+        for i, unit in enumerate(units[:first]):
+            transpose(unit)
+            empty(unit, 0)
+            empty(unit, 1)
+            quantise(unit)
+            if i >= first - 2:
+                make_table(gains[i - (first - 2)])
+
+        done = first
+        for step in range(STEPS):
+            g, j = divmod(step, TOKEN_TILES)
+            ahead = units[done : done + (2 if step < TOKEN_TILES - 1 else 1)]
+            done += len(ahead)
+            if j == 0:
+                result = ring.tile([P, HEADS, TOKEN_TILES, D], F32, name="result")
+            acc = multiply(g, j)
+            sums = sum_squares(acc)
+            for unit in ahead[:1]:
+                transpose(unit)
+                empty(unit, 0)
+            inv = inverse_rms(sums)
+            for unit in ahead[:1]:
+                empty(unit, 1)
+            if g == V_GROUP:
+                nc.vector.tensor_tensor(
+                    out=result[:, :, j, :], in0=acc[:], in1=inv[:].to_broadcast([P, HEADS, D]), op=ALU.mult
+                )
+                if j >= 1:
+                    store(g, result, 0 if j == 1 else j, j + 1)
+                continue
+            terms = products(acc, inv, tables[g // K_GROUP], j)
+            for unit in ahead[:1]:
+                quantise(unit)
+            add_terms(terms, result, j)
+            for unit in ahead[1:]:
+                transpose(unit)
+                empty(unit, 0)
+                empty(unit, 1)
+                quantise(unit)
+            if j == TOKEN_TILES - 1:
+                store(g, result, 0, TOKEN_TILES)

@@ -21,6 +21,7 @@ K_PASS = 512
 PASSES = HID // K_PASS
 TOKEN_TILES = S // P
 HEADS = 4
+N = HEADS * D
 GROUPS = (H + 2 * KV) // HEADS
 K_GROUP = H // HEADS
 V_GROUP = K_GROUP + 1
@@ -32,7 +33,7 @@ def tile_refattention_pa_kernel(
     tc, hidden_states, cos, sin, Wq, Wk, Wv, q_norm_w, k_norm_w, out_0, out_1, out_2
 ):
     nc = tc.nc
-    weights = [Wq[g * HEADS * D : (g + 1) * HEADS * D, :] for g in range(K_GROUP)] + [Wk, Wv]
+    weights = [Wq[g * N : (g + 1) * N, :] for g in range(K_GROUP)] + [Wk, Wv]
     outs = [out_0[0, g * HEADS : (g + 1) * HEADS] for g in range(K_GROUP)] + [out_1[0], out_2[0]]
 
     with ExitStack() as ctx:
@@ -50,72 +51,69 @@ def tile_refattention_pa_kernel(
         ident = keep.tile([P, P], F32)
         make_identity(nc, ident[:])
 
-        blocks = {}
         x_rows = hidden_states[0].rearrange("(p j) k -> p j k", j=TOKEN_TILES)
 
-        def load_x(j):
-            raw = keep.tile([P, HID], BF16, name="x_raw%d" % j)
-            nc.sync.dma_start(out=raw[:], in_=x_rows[:, j, :])
-            words = raw[:].bitcast(F32)
-            blocks[("x", j)] = [words[:, c * WORDS : (c + 1) * WORDS] for c in range(PASSES)]
+        def load(name, rows):
+            raw = keep.tile(list(rows.shape), BF16, name=name)
+            nc.sync.dma_start(out=raw[:], in_=rows)
+            return [
+                [raw[:, a, :].bitcast(F32)[:, c * WORDS : (c + 1) * WORDS] for c in range(rows.shape[2] // K_PASS)]
+                for a in range(rows.shape[1])
+            ]
 
-        def load_w(g, c0, n):
-            raw = keep.tile([P, HEADS, n * K_PASS], BF16, name="w_raw%d_%d" % (g, c0))
-            rows = weights[g].rearrange("(h p) k -> p h k", p=P)
-            nc.sync.dma_start(out=raw[:], in_=rows[:, :, c0 * K_PASS : (c0 + n) * K_PASS])
-            for c in range(n):
-                blocks[("w", g, c0 + c)] = [
-                    raw[:, h, :].bitcast(F32)[:, c * WORDS : (c + 1) * WORDS] for h in range(HEADS)
-                ]
+        def load_rows(name, rows):
+            return [block for row_tile in load(name, rows) for block in row_tile]
 
+        def load_pair(g, pair):
+            rows = weights[g].rearrange("(h p) k -> p h k", p=P)[:, :, 2 * pair * K_PASS : 2 * (pair + 1) * K_PASS]
+            by_head = load("w_raw%d_%d" % (g, pair), rows)
+            return [by_head[h][c] for c in range(2) for h in range(HEADS)]
+
+        w0_rows = weights[0].rearrange("(h p) k -> p h k", p=P)
+        head_runs = [load_rows("x_raw0", x_rows[:, 0:1, :])]
+        head_runs += [load_rows("w_raw0_%d" % h, w0_rows[:, h : h + 1, :]) for h in range(HEADS)]
+        head_runs += [load_rows("x_raw1", x_rows[:, 1:2, :])]
         cos_sb = keep.tile([P, TOKEN_TILES, D], BF16)
         sin_sb = keep.tile([P, TOKEN_TILES, D], BF16)
-        load_w(0, 0, 1)
-        load_x(0)
-        for c in range(1, PASSES):
-            load_w(0, c, 1)
-        load_x(1)
         nc.sync.dma_start(out=cos_sb[:], in_=cos[0].rearrange("(p j) d -> p j d", j=TOKEN_TILES))
         nc.sync.dma_start(out=sin_sb[:], in_=sin[0].rearrange("(p j) d -> p j d", j=TOKEN_TILES))
-        load_w(1, 0, 1)
-        load_x(2)
-        load_w(1, 1, 1)
-        load_x(3)
-        load_w(1, 2, 2)
-        for g in range(2, GROUPS):
-            load_w(g, 0, 2)
-            load_w(g, 2, 2)
+        x_rest = load_rows("x_raw2", x_rows[:, 2:, :])
+        w_runs = {(g, pair): load_pair(g, pair) for g in range(1, GROUPS) for pair in range(2)}
 
-        units = [("w", 0, 0), ("x", 0), ("w", 0, 1), ("w", 0, 2), ("w", 0, 3), ("x", 1)]
-        units += [("w", 1, 0), ("x", 2), ("w", 1, 1), ("x", 3), ("w", 1, 2), ("w", 1, 3)]
-        units += [("w", g, c) for g in range(2, GROUPS) for c in range(PASSES)]
-
-        banks, grouped, quantised = {}, {}, {}
-
-        def transpose(unit):
-            banks[unit] = []
-            for half in range(2):
+        def transpose(blocks):
+            banks = []
+            for first in range(0, len(blocks), 2):
                 bank = psum.tile([P, 2, 2, P], F32, name="turned")
                 for a in range(2):
                     for u in range(2):
-                        nc.tensor.transpose(bank[:, a, u, :], blocks[unit][2 * half + a][:, u:WORDS:2], ident[:])
-                banks[unit].append(bank)
-            staged = ring.tile([P, 4 * K_PASS], BF16, name="grouped", align_bytes=64)
-            grouped[unit] = staged
+                        nc.tensor.transpose(bank[:, a, u, :], blocks[first + a][:, u:WORDS:2], ident[:])
+                banks.append(bank)
+            grouped = ring.tile([P, len(blocks) * K_PASS], BF16, name="grouped", align_bytes=256)
+            return banks, grouped
 
-        def empty(unit, half):
-            words = grouped[unit][:].bitcast(F32)[:, half * 2 * WORDS : (half + 1) * 2 * WORDS]
+        def empty(banks, grouped, i):
+            words = grouped[:].bitcast(F32)[:, i * 2 * WORDS : (i + 1) * 2 * WORDS]
             nc.scalar.copy(
                 out=words.rearrange("p (a r u) -> p a r u", a=2, u=2),
-                in_=banks[unit][half][:].rearrange("p a u r -> p a r u"),
+                in_=banks[i][:].rearrange("p a u r -> p a r u"),
             )
 
-        def quantise(unit):
-            kind, bufs = ("x", TOKEN_TILES) if unit[0] == "x" else ("w", 2 * PASSES)
-            codes = ring.tile([P, K_PASS], U32, name=kind + "_codes", bufs=bufs, align_bytes=64)
-            scales = ring.tile([P, K_PASS], U8, name=kind + "_scales", bufs=bufs, align_bytes=64)
-            nc.vector.quantize_mx(out=codes[:].bitcast(E5M2X4), scales=scales[:], in_=grouped[unit][:])
-            quantised[unit] = (codes, scales)
+        def quantise(codes, scales, values):
+            nc.vector.quantize_mx(out=codes.bitcast(E5M2X4), scales=scales, in_=values)
+
+        x_codes = keep.tile([P, TOKEN_TILES * PASSES * P], U32, align_bytes=256)
+        x_scales = keep.tile([P, TOKEN_TILES * PASSES * P], U8, align_bytes=256)
+        w_mx = {}
+
+        def new_w_pair(g, pair):
+            w_codes = ring.tile([P, 2 * N], U32, name="w_codes", bufs=4, align_bytes=256)
+            w_scales = ring.tile([P, 2 * N], U8, name="w_scales", bufs=4, align_bytes=256)
+            w_mx[(g, pair)] = (w_codes, w_scales)
+            return w_codes, w_scales
+
+        def quantise_x(grouped, j0, j1):
+            cols = slice(j0 * PASSES * P, j1 * PASSES * P)
+            quantise(x_codes[:, cols], x_scales[:, cols], grouped[:])
 
         tables = []
 
@@ -140,103 +138,138 @@ def tile_refattention_pa_kernel(
             )
             tables.append(table)
 
-        def multiply(g, j):
-            acc = psum.tile([P, HEADS, D], F32, name="acc")
-            x_codes, x_scales = quantised[("x", j)]
+        def multiply(g, j, h0, h1):
+            acc = psum.tile([P, h1 - h0, D], F32, name="acc")
             for c in range(PASSES):
-                w_codes, w_scales = quantised[("w", g, c)]
+                w_codes, w_scales = w_mx[(g, c // 2)]
+                x_cols = slice((j * PASSES + c) * P, (j * PASSES + c + 1) * P)
+                w_cols = slice((c % 2) * N + h0 * D, (c % 2) * N + h1 * D)
                 nc.tensor.matmul_mx(
                     out=acc[:].rearrange("p h d -> p (h d)"),
-                    lhsT=x_codes[:, c * P : (c + 1) * P].bitcast(E5M2X4),
-                    lhsT_scale=x_scales[:, c * P : (c + 1) * P],
-                    rhs=w_codes[:].bitcast(E5M2X4),
-                    rhs_scale=w_scales[:],
+                    lhsT=x_codes[:, x_cols].bitcast(E5M2X4),
+                    lhsT_scale=x_scales[:, x_cols],
+                    rhs=w_codes[:, w_cols].bitcast(E5M2X4),
+                    rhs_scale=w_scales[:, w_cols],
                     start=(c == 0),
                     stop=(c == PASSES - 1),
                 )
             return acc
 
         def sum_squares(acc):
-            sums = ring.tile([P, HEADS], F32, name="sums")
-            squares = ring.tile([P, HEADS, D], F32, name="squares", bufs=2)
-            for h in range(HEADS):
+            heads = acc.shape[1]
+            sums = ring.tile([P, heads], F32, name="sums")
+            squares = ring.tile([P, heads, D], F32, name="squares", bufs=1)
+            for h in range(heads):
                 nc.scalar.activation(
                     out=squares[:, h, :], in_=acc[:, h, :], func=ACT.Square, accum_out=sums[:, h : h + 1]
                 )
             return sums
 
         def inverse_rms(sums):
-            inv = ring.tile([P, HEADS, 1], F32, name="inv")
+            inv = ring.tile([P, sums.shape[1], 1], F32, name="inv")
             nc.scalar.activation(out=inv[:, :, 0], in_=sums[:], func=ACT.Abs_reciprocal_sqrt, scale=1.0 / D, bias=EPS)
             return inv
 
-        def products(acc, inv, table, j):
-            terms = ring.tile([P, HEADS, 2, D], F32, name="terms", bufs=2)
+        results = {}
+
+        def store(g, h0, h1, j0, j1):
+            dest = outs[g].rearrange("h (p j) d -> p h (j d)", j=TOKEN_TILES)
+            nc.sync.dma_start(
+                out=dest[:, h0:h1, j0 * D : j1 * D],
+                in_=results[g][:].rearrange("p h j d -> p h (j d)")[:, h0:h1, j0 * D : j1 * D],
+            )
+
+        def result_of(g):
+            if g not in results:
+                results[g] = ring.tile([P, HEADS, TOKEN_TILES, D], F32, name="result", bufs=4)
+            return results[g]
+
+        def products(step, acc, inv):
+            g, j = divmod(step, TOKEN_TILES)
+            terms = ring.tile([P, HEADS, 2, D], F32, name="terms")
             for h in range(HEADS):
                 nc.vector.scalar_tensor_tensor(
                     out=terms[:, h, :, :],
                     in0=acc[:, h : h + 1, :].to_broadcast([P, 2, D]),
                     scalar=inv[:, h, :],
-                    in1=table[:, j, :, :],
+                    in1=tables[g // K_GROUP][:, j, :, :],
                     op0=ALU.mult,
                     op1=ALU.mult,
                 )
             return terms
 
-        def add_terms(terms, result, j):
-            nc.vector.tensor_tensor(
-                out=result[:, :, j, :].rearrange("p h (t i) -> p h t i", t=2),
+        def add_terms(step, terms):
+            g, j = divmod(step, TOKEN_TILES)
+            nc.gpsimd.tensor_tensor(
+                out=result_of(g)[:, :, j, :].rearrange("p h (t i) -> p h t i", t=2),
                 in0=terms[:, :, 0, :].rearrange("p h (t i) -> p h t i", t=2),
                 in1=terms[:, :, 1, :].rearrange("p h (t i) -> p h t i", t=2)[:, :, ::-1, :],
                 op=ALU.add,
             )
+            if g == K_GROUP and j >= 1:
+                store(g, 0, HEADS, 0 if j == 1 else j, j + 1)
+            elif j == TOKEN_TILES - 1:
+                store(g, 0, HEADS, 0, TOKEN_TILES)
 
-        def store(g, result, j0, j1):
-            dest = outs[g].rearrange("h (p j) d -> p h (j d)", j=TOKEN_TILES)
-            nc.sync.dma_start(
-                out=dest[:, :, j0 * D : j1 * D],
-                in_=result[:].rearrange("p h j d -> p h (j d)")[:, :, j0 * D : j1 * D],
+        def normalise_v(acc, inv, j, h0, h1):
+            nc.vector.tensor_tensor(
+                out=result_of(V_GROUP)[:, h0:h1, j, :],
+                in0=acc[:],
+                in1=inv[:].to_broadcast([P, h1 - h0, D]),
+                op=ALU.mult,
             )
 
-        first = PASSES + 2
-        for i, unit in enumerate(units[:first]):
-            transpose(unit)
-            empty(unit, 0)
-            empty(unit, 1)
-            quantise(unit)
-            if i >= first - 2:
-                make_table(gains[i - (first - 2)])
+        for pair in range(2):
+            new_w_pair(0, pair)
+        for i, blocks in enumerate(head_runs):
+            banks, grouped = transpose(blocks)
+            empty(banks, grouped, 0)
+            empty(banks, grouped, 1)
+            if i == 0 or i == HEADS + 1:
+                j = i // (HEADS + 1)
+                quantise_x(grouped, j, j + 1)
+            else:
+                for c in range(PASSES):
+                    w_codes, w_scales = w_mx[(0, c // 2)]
+                    cols = slice((c % 2) * N + (i - 1) * D, (c % 2) * N + i * D)
+                    quantise(w_codes[:, cols], w_scales[:, cols], grouped[:, c * K_PASS : (c + 1) * K_PASS])
+        for gain in gains:
+            make_table(gain)
 
-        done = first
-        for step in range(STEPS):
+        run_after = {0: "x", 1: (1, 0), 2: (1, 1)}
+        for g in range(2, GROUPS):
+            for pair in range(2):
+                run_after[(g - 1) * TOKEN_TILES - 1 + 2 * pair] = (g, pair)
+
+        for step in range(V_GROUP * TOKEN_TILES):
             g, j = divmod(step, TOKEN_TILES)
-            ahead = units[done : done + (2 if step < TOKEN_TILES - 1 else 1)]
-            done += len(ahead)
-            if j == 0:
-                result = ring.tile([P, HEADS, TOKEN_TILES, D], F32, name="result")
-            acc = multiply(g, j)
+            acc = multiply(g, j, 0, HEADS)
             sums = sum_squares(acc)
-            for unit in ahead[:1]:
-                transpose(unit)
-                empty(unit, 0)
-            inv = inverse_rms(sums)
-            for unit in ahead[:1]:
-                empty(unit, 1)
-            if g == V_GROUP:
-                nc.vector.tensor_tensor(
-                    out=result[:, :, j, :], in0=acc[:], in1=inv[:].to_broadcast([P, HEADS, D]), op=ALU.mult
-                )
-                if j >= 1:
-                    store(g, result, 0 if j == 1 else j, j + 1)
+            run = run_after.get(step)
+            if run is None:
+                add_terms(step, products(step, acc, inverse_rms(sums)))
                 continue
-            terms = products(acc, inv, tables[g // K_GROUP], j)
-            for unit in ahead[:1]:
-                quantise(unit)
-            add_terms(terms, result, j)
-            for unit in ahead[1:]:
-                transpose(unit)
-                empty(unit, 0)
-                empty(unit, 1)
-                quantise(unit)
-            if j == TOKEN_TILES - 1:
-                store(g, result, 0, TOKEN_TILES)
+            banks, grouped = transpose(x_rest if run == "x" else w_runs[run])
+            empty(banks, grouped, 0)
+            inv = inverse_rms(sums)
+            for i in range(1, len(banks)):
+                empty(banks, grouped, i)
+            terms = products(step, acc, inv)
+            if run == "x":
+                quantise_x(grouped, 2, TOKEN_TILES)
+            else:
+                w_codes, w_scales = new_w_pair(*run)
+                quantise(w_codes[:], w_scales[:], grouped[:])
+            add_terms(step, terms)
+
+        for j in range(TOKEN_TILES - 1):
+            acc = multiply(V_GROUP, j, 0, HEADS)
+            normalise_v(acc, inverse_rms(sum_squares(acc)), j, 0, HEADS)
+            if j >= 1:
+                store(V_GROUP, 0, HEADS, 0 if j == 1 else j, j + 1)
+        j = TOKEN_TILES - 1
+        for h0 in (0, HEADS // 2):
+            h1 = h0 + HEADS // 2
+            acc = multiply(V_GROUP, j, h0, h1)
+            normalise_v(acc, inverse_rms(sum_squares(acc)), j, h0, h1)
+            store(V_GROUP, h0, h1, j, j + 1)

@@ -1,4 +1,5 @@
 from contextlib import ExitStack
+from functools import partial
 
 import concourse.mybir as mybir
 from concourse.masks import make_identity
@@ -42,11 +43,12 @@ def tile_refattention_pa_kernel(
         psum = ctx.enter_context(tc.psum_pool(name="psum", bufs=4))
         ctx.enter_context(tc.manual_schedule())
 
-        gains = []
-        for name, gain in (("q_gain", q_norm_w), ("k_gain", k_norm_w)):
-            spread = keep.tile([P, 1, D], BF16, name=name)
-            nc.scalar.dma_start(out=spread[:, 0, :], in_=gain.partition_broadcast(P))
-            gains.append(spread)
+        gain_rows = keep.tile([P, 2, D], BF16)
+        ones = keep.tile([P, P], BF16)
+        nc.vector.memset(gain_rows[:], 0.0)
+        nc.vector.memset(ones[:], 1.0)
+        for t, gain in enumerate((q_norm_w, k_norm_w)):
+            nc.scalar.dma_start(out=gain_rows[0:1, t, :], in_=gain.rearrange("(o d) -> o d", o=1))
 
         ident = keep.tile([P, P], F32)
         make_identity(nc, ident[:])
@@ -70,14 +72,16 @@ def tile_refattention_pa_kernel(
             return [by_head[h][c] for c in range(2) for h in range(HEADS)]
 
         w0_rows = weights[0].rearrange("(h p) k -> p h k", p=P)
-        head_runs = [load_rows("x_raw0", x_rows[:, 0:1, :])]
-        head_runs += [load_rows("w_raw0_%d" % h, w0_rows[:, h : h + 1, :]) for h in range(HEADS)]
-        head_runs += [load_rows("x_raw1", x_rows[:, 1:2, :])]
+        head_order = [("x", 0), ("w", 0), ("x", 1), ("w", 1), ("w", 2), ("w", 3)]
+        head_runs = [
+            load_rows("%s_raw%d" % (kind, i), (x_rows if kind == "x" else w0_rows)[:, i : i + 1, :])
+            for kind, i in head_order
+        ]
+        x_rest = load_rows("x_raw2", x_rows[:, 2:3, :]) + load_rows("x_raw3", x_rows[:, 3:4, :])
         cos_sb = keep.tile([P, TOKEN_TILES, D], BF16)
         sin_sb = keep.tile([P, TOKEN_TILES, D], BF16)
         nc.sync.dma_start(out=cos_sb[:], in_=cos[0].rearrange("(p j) d -> p j d", j=TOKEN_TILES))
         nc.sync.dma_start(out=sin_sb[:], in_=sin[0].rearrange("(p j) d -> p j d", j=TOKEN_TILES))
-        x_rest = load_rows("x_raw2", x_rows[:, 2:, :])
         w_runs = {(g, pair): load_pair(g, pair) for g in range(1, GROUPS) for pair in range(2)}
 
         def transpose(blocks):
@@ -91,9 +95,9 @@ def tile_refattention_pa_kernel(
             grouped = ring.tile([P, len(blocks) * K_PASS], BF16, name="grouped", align_bytes=256)
             return banks, grouped
 
-        def empty(banks, grouped, i):
+        def empty(copy, banks, grouped, i):
             words = grouped[:].bitcast(F32)[:, i * 2 * WORDS : (i + 1) * 2 * WORDS]
-            nc.scalar.copy(
+            copy(
                 out=words.rearrange("p (a r u) -> p a r u", a=2, u=2),
                 in_=banks[i][:].rearrange("p a u r -> p a r u"),
             )
@@ -120,7 +124,7 @@ def tile_refattention_pa_kernel(
         def make_table(gain):
             table = keep.tile([P, TOKEN_TILES, 2, D], F32, name="table%d" % len(tables))
             nc.vector.tensor_tensor(
-                out=table[:, :, 0, :], in0=cos_sb[:], in1=gain[:].to_broadcast([P, TOKEN_TILES, D]), op=ALU.mult
+                out=table[:, :, 0, :], in0=cos_sb[:], in1=gain.to_broadcast([P, TOKEN_TILES, D]), op=ALU.mult
             )
             nc.vector.tensor_tensor(
                 out=table[:, :, 1, :HALF],
@@ -138,31 +142,37 @@ def tile_refattention_pa_kernel(
             )
             tables.append(table)
 
-        def multiply(g, j, h0, h1):
-            acc = psum.tile([P, h1 - h0, D], F32, name="acc")
-            for c in range(PASSES):
-                w_codes, w_scales = w_mx[(g, c // 2)]
-                x_cols = slice((j * PASSES + c) * P, (j * PASSES + c + 1) * P)
-                w_cols = slice((c % 2) * N + h0 * D, (c % 2) * N + h1 * D)
-                nc.tensor.matmul_mx(
-                    out=acc[:].rearrange("p h d -> p (h d)"),
-                    lhsT=x_codes[:, x_cols].bitcast(E5M2X4),
-                    lhsT_scale=x_scales[:, x_cols],
-                    rhs=w_codes[:, w_cols].bitcast(E5M2X4),
-                    rhs_scale=w_scales[:, w_cols],
-                    start=(c == 0),
-                    stop=(c == PASSES - 1),
-                )
+        def multiply(g, heads, tiles):
+            acc = psum.tile([P, len(tiles), len(heads), D], F32, name="turned" if g == V_GROUP else "acc")
+            for i, j in enumerate(tiles):
+                for c in range(PASSES):
+                    w_codes, w_scales = w_mx[(g, c // 2)]
+                    x_cols = slice((j * PASSES + c) * P, (j * PASSES + c + 1) * P)
+                    w_cols = slice((c % 2) * N + heads.start * D, (c % 2) * N + heads.stop * D)
+                    nc.tensor.matmul_mx(
+                        out=acc[:, i, :, :].rearrange("p h d -> p (h d)"),
+                        lhsT=x_codes[:, x_cols].bitcast(E5M2X4),
+                        lhsT_scale=x_scales[:, x_cols],
+                        rhs=w_codes[:, w_cols].bitcast(E5M2X4),
+                        rhs_scale=w_scales[:, w_cols],
+                        start=(c == 0),
+                        stop=(c == PASSES - 1),
+                    )
             return acc
 
+        waiting = []
+
         def sum_squares(acc):
-            heads = acc.shape[1]
-            sums = ring.tile([P, heads], F32, name="sums")
-            squares = ring.tile([P, heads, D], F32, name="squares", bufs=1)
-            for h in range(heads):
+            rows = acc[:].rearrange("p j h d -> p (j h) d")
+            count = rows.shape[1]
+            sums = ring.tile([P, count], F32, name="sums")
+            squares = ring.tile([P, count, D], F32, name="squares", bufs=2)
+            for r in range(count):
                 nc.scalar.activation(
-                    out=squares[:, h, :], in_=acc[:, h, :], func=ACT.Square, accum_out=sums[:, h : h + 1]
+                    out=squares[:, r, :], in_=rows[:, r, :], func=ACT.Square, accum_out=sums[:, r : r + 1]
                 )
+                while waiting:
+                    waiting.pop()()
             return sums
 
         def inverse_rms(sums):
@@ -170,106 +180,114 @@ def tile_refattention_pa_kernel(
             nc.scalar.activation(out=inv[:, :, 0], in_=sums[:], func=ACT.Abs_reciprocal_sqrt, scale=1.0 / D, bias=EPS)
             return inv
 
-        results = {}
-
-        def store(g, h0, h1, j0, j1):
+        def store(g, heads, tiles, result):
             dest = outs[g].rearrange("h (p j) d -> p h (j d)", j=TOKEN_TILES)
             nc.sync.dma_start(
-                out=dest[:, h0:h1, j0 * D : j1 * D],
-                in_=results[g][:].rearrange("p h j d -> p h (j d)")[:, h0:h1, j0 * D : j1 * D],
+                out=dest[:, heads.start : heads.stop, tiles.start * D : tiles.stop * D],
+                in_=result[:].rearrange("p h j d -> p h (j d)"),
             )
 
-        def result_of(g):
-            if g not in results:
-                results[g] = ring.tile([P, HEADS, TOKEN_TILES, D], F32, name="result", bufs=4)
-            return results[g]
+        def new_result(heads, tiles):
+            result = ring.tile([P, len(heads), len(tiles), D], F32, name="result", bufs=14)
+            return result
 
-        def products(step, acc, inv):
-            g, j = divmod(step, TOKEN_TILES)
-            terms = ring.tile([P, HEADS, 2, D], F32, name="terms")
-            for h in range(HEADS):
-                nc.vector.scalar_tensor_tensor(
-                    out=terms[:, h, :, :],
-                    in0=acc[:, h : h + 1, :].to_broadcast([P, 2, D]),
-                    scalar=inv[:, h, :],
-                    in1=tables[g // K_GROUP][:, j, :, :],
-                    op0=ALU.mult,
-                    op1=ALU.mult,
-                )
+        def products(g, heads, tiles, acc, inv):
+            terms = ring.tile([P, len(heads), len(tiles), 2, D], F32, name="terms")
+            for i, j in enumerate(tiles):
+                for h in range(len(heads)):
+                    nc.vector.scalar_tensor_tensor(
+                        out=terms[:, h, i, :, :],
+                        in0=acc[:, i, h : h + 1, :].to_broadcast([P, 2, D]),
+                        scalar=inv[:, i * len(heads) + h, :],
+                        in1=tables[g // K_GROUP][:, j, :, :],
+                        op0=ALU.mult,
+                        op1=ALU.mult,
+                    )
             return terms
 
-        def add_terms(step, terms):
-            g, j = divmod(step, TOKEN_TILES)
-            nc.gpsimd.tensor_tensor(
-                out=result_of(g)[:, :, j, :].rearrange("p h (t i) -> p h t i", t=2),
-                in0=terms[:, :, 0, :].rearrange("p h (t i) -> p h t i", t=2),
-                in1=terms[:, :, 1, :].rearrange("p h (t i) -> p h t i", t=2)[:, :, ::-1, :],
+        def add_terms(engine, g, heads, tiles, terms):
+            result = new_result(heads, tiles)
+            halves = terms[:].rearrange("p h j s (t i) -> p (h j) s t i", t=2)
+            engine.tensor_tensor(
+                out=result[:].rearrange("p h j (t i) -> p (h j) t i", t=2),
+                in0=halves[:, :, 0, :, :],
+                in1=halves[:, :, 1, ::-1, :],
                 op=ALU.add,
             )
-            if g == K_GROUP and j >= 1:
-                store(g, 0, HEADS, 0 if j == 1 else j, j + 1)
-            elif j == TOKEN_TILES - 1:
-                store(g, 0, HEADS, 0, TOKEN_TILES)
+            store(g, heads, tiles, result)
 
-        def normalise_v(acc, inv, j, h0, h1):
+        def finish_rotary(piece, acc, sums):
+            engine = nc.vector if piece == last_rotary else nc.gpsimd
+            add_terms(engine, *piece, products(*piece, acc, inverse_rms(sums)))
+
+        def finish_v(piece, acc, sums):
+            g, heads, tiles = piece
+            inv = inverse_rms(sums)
+            result = new_result(heads, tiles)
             nc.vector.tensor_tensor(
-                out=result_of(V_GROUP)[:, h0:h1, j, :],
+                out=result[:].rearrange("p h j d -> p j h d"),
                 in0=acc[:],
-                in1=inv[:].to_broadcast([P, h1 - h0, D]),
+                in1=inv[:].rearrange("p (j h) o -> p j h o", h=len(heads)).to_broadcast([P, len(tiles), len(heads), D]),
                 op=ALU.mult,
             )
+            store(g, heads, tiles, result)
 
         for pair in range(2):
             new_w_pair(0, pair)
-        for i, blocks in enumerate(head_runs):
+        for (kind, i), blocks in zip(head_order, head_runs):
             banks, grouped = transpose(blocks)
-            empty(banks, grouped, 0)
-            empty(banks, grouped, 1)
-            if i == 0 or i == HEADS + 1:
-                j = i // (HEADS + 1)
-                quantise_x(grouped, j, j + 1)
+            empty(nc.vector.tensor_copy if kind == "x" else nc.scalar.copy, banks, grouped, 0)
+            empty(nc.scalar.copy, banks, grouped, 1)
+            if kind == "x":
+                quantise_x(grouped, i, i + 1)
             else:
                 for c in range(PASSES):
                     w_codes, w_scales = w_mx[(0, c // 2)]
-                    cols = slice((c % 2) * N + (i - 1) * D, (c % 2) * N + i * D)
+                    cols = slice((c % 2) * N + i * D, (c % 2) * N + (i + 1) * D)
                     quantise(w_codes[:, cols], w_scales[:, cols], grouped[:, c * K_PASS : (c + 1) * K_PASS])
-        for gain in gains:
-            make_table(gain)
+        gains = psum.tile([P, 2, D], F32, name="acc")
+        nc.tensor.matmul(
+            gains[:].rearrange("p t d -> p (t d)"),
+            lhsT=ones[:],
+            rhs=gain_rows[:].rearrange("p t d -> p (t d)"),
+            start=True,
+            stop=True,
+        )
+        for t in range(2):
+            make_table(gains[:, t : t + 1, :])
 
         run_after = {0: "x", 1: (1, 0), 2: (1, 1)}
         for g in range(2, GROUPS):
             for pair in range(2):
                 run_after[(g - 1) * TOKEN_TILES - 1 + 2 * pair] = (g, pair)
 
-        for step in range(V_GROUP * TOKEN_TILES):
-            g, j = divmod(step, TOKEN_TILES)
-            acc = multiply(g, j, 0, HEADS)
+        pieces = [
+            (g, range(h, h + 2), range(j, j + 2))
+            for g in range(GROUPS)
+            for j in range(0, TOKEN_TILES, 2)
+            for h in range(0, HEADS, 2)
+        ]
+        last_rotary = pieces[V_GROUP * TOKEN_TILES - 1]
+        g, heads, tiles = pieces.pop()
+        pieces += [(g, heads, range(j, j + 1)) for j in tiles]
+
+        for step, piece in enumerate(pieces):
+            acc = multiply(*piece)
             sums = sum_squares(acc)
             run = run_after.get(step)
             if run is None:
-                add_terms(step, products(step, acc, inverse_rms(sums)))
+                waiting.append(partial(finish_v if piece[0] == V_GROUP else finish_rotary, piece, acc, sums))
                 continue
             banks, grouped = transpose(x_rest if run == "x" else w_runs[run])
-            empty(banks, grouped, 0)
+            empty(nc.vector.tensor_copy, banks, grouped, 0)
             inv = inverse_rms(sums)
             for i in range(1, len(banks)):
-                empty(banks, grouped, i)
-            terms = products(step, acc, inv)
+                empty(nc.scalar.copy, banks, grouped, i)
+            terms = products(*piece, acc, inv)
             if run == "x":
                 quantise_x(grouped, 2, TOKEN_TILES)
             else:
                 w_codes, w_scales = new_w_pair(*run)
                 quantise(w_codes[:], w_scales[:], grouped[:])
-            add_terms(step, terms)
-
-        for j in range(TOKEN_TILES - 1):
-            acc = multiply(V_GROUP, j, 0, HEADS)
-            normalise_v(acc, inverse_rms(sum_squares(acc)), j, 0, HEADS)
-            if j >= 1:
-                store(V_GROUP, 0, HEADS, 0 if j == 1 else j, j + 1)
-        j = TOKEN_TILES - 1
-        for h0 in (0, HEADS // 2):
-            h1 = h0 + HEADS // 2
-            acc = multiply(V_GROUP, j, h0, h1)
-            normalise_v(acc, inverse_rms(sum_squares(acc)), j, h0, h1)
-            store(V_GROUP, h0, h1, j, j + 1)
+            add_terms(nc.gpsimd, *piece, terms)
+        waiting.pop()()

@@ -50,6 +50,9 @@ def tile_refattention_pa_kernel(
         for t, gain in enumerate((q_norm_w, k_norm_w)):
             nc.scalar.dma_start(out=gain_rows[0:1, t, :], in_=gain.rearrange("(o d) -> o d", o=1))
 
+        unread = keep.tile([P, 1], F32)
+        nc.scalar.activation(out=unread[:], in_=ones[:, 0:1], func=ACT.Abs_reciprocal_sqrt)
+
         ident = keep.tile([P, P], F32)
         make_identity(nc, ident[:])
 

from contextlib import ExitStack
from functools import partial

import concourse.mybir as mybir
from concourse.masks import make_identity

S, HID, H, KV, D = 512, 2048, 16, 4, 128
EPS = 1e-6
HALF = D // 2
FLOPS = 2 * S * HID * (H + 2 * KV) * D

F32 = mybir.dt.float32
BF16 = mybir.dt.bfloat16
U32 = mybir.dt.uint32
U8 = mybir.dt.uint8
E5M2X4 = mybir.dt.float8_e5m2_x4
ACT = mybir.ActivationFunctionType
ALU = mybir.AluOpType

P = 128
K_PASS = 512
PASSES = HID // K_PASS
TOKEN_TILES = S // P
HEADS = 4
N = HEADS * D
GROUPS = (H + 2 * KV) // HEADS
K_GROUP = H // HEADS
V_GROUP = K_GROUP + 1
WORDS = K_PASS // 2
STEPS = GROUPS * TOKEN_TILES


def tile_refattention_pa_kernel(
    tc, hidden_states, cos, sin, Wq, Wk, Wv, q_norm_w, k_norm_w, out_0, out_1, out_2
):
    nc = tc.nc
    weights = [Wq[g * N : (g + 1) * N, :] for g in range(K_GROUP)] + [Wk, Wv]
    outs = [out_0[0, g * HEADS : (g + 1) * HEADS] for g in range(K_GROUP)] + [out_1[0], out_2[0]]

    with ExitStack() as ctx:
        keep = ctx.enter_context(tc.tile_pool(name="keep", bufs=1))
        ring = ctx.enter_context(tc.tile_pool(name="ring", bufs=3))
        psum = ctx.enter_context(tc.psum_pool(name="psum", bufs=4))
        ctx.enter_context(tc.manual_schedule())

        gain_rows = keep.tile([P, 2, D], BF16)
        ones = keep.tile([P, P], BF16)
        nc.vector.memset(gain_rows[:], 0.0)
        nc.vector.memset(ones[:], 1.0)
        for t, gain in enumerate((q_norm_w, k_norm_w)):
            nc.scalar.dma_start(out=gain_rows[0:1, t, :], in_=gain.rearrange("(o d) -> o d", o=1))

        unread = keep.tile([P, 1], F32)
        nc.scalar.activation(out=unread[:], in_=ones[:, 0:1], func=ACT.Abs_reciprocal_sqrt)

        ident = keep.tile([P, P], F32)
        make_identity(nc, ident[:])

        x_rows = hidden_states[0].rearrange("(p j) k -> p j k", j=TOKEN_TILES)

        def load(name, rows):
            raw = keep.tile(list(rows.shape), BF16, name=name)
            nc.sync.dma_start(out=raw[:], in_=rows)
            return [
                [raw[:, a, :].bitcast(F32)[:, c * WORDS : (c + 1) * WORDS] for c in range(rows.shape[2] // K_PASS)]
                for a in range(rows.shape[1])
            ]

        def load_rows(name, rows):
            return [block for row_tile in load(name, rows) for block in row_tile]

        def load_pair(g, pair):
            rows = weights[g].rearrange("(h p) k -> p h k", p=P)[:, :, 2 * pair * K_PASS : 2 * (pair + 1) * K_PASS]
            by_head = load("w_raw%d_%d" % (g, pair), rows)
            return [by_head[h][c] for c in range(2) for h in range(HEADS)]

        w0_rows = weights[0].rearrange("(h p) k -> p h k", p=P)
        head_order = [("x", 0), ("w", 0), ("x", 1), ("w", 1), ("w", 2), ("w", 3)]
        head_runs = [
            load_rows("%s_raw%d" % (kind, i), (x_rows if kind == "x" else w0_rows)[:, i : i + 1, :])
            for kind, i in head_order
        ]
        x_rest = load_rows("x_raw2", x_rows[:, 2:3, :]) + load_rows("x_raw3", x_rows[:, 3:4, :])
        cos_sb = keep.tile([P, TOKEN_TILES, D], BF16)
        sin_sb = keep.tile([P, TOKEN_TILES, D], BF16)
        nc.sync.dma_start(out=cos_sb[:], in_=cos[0].rearrange("(p j) d -> p j d", j=TOKEN_TILES))
        nc.sync.dma_start(out=sin_sb[:], in_=sin[0].rearrange("(p j) d -> p j d", j=TOKEN_TILES))
        w_runs = {(g, pair): load_pair(g, pair) for g in range(1, GROUPS) for pair in range(2)}

        def transpose(blocks):
            banks = []
            for first in range(0, len(blocks), 2):
                bank = psum.tile([P, 2, 2, P], F32, name="turned")
                for a in range(2):
                    for u in range(2):
                        nc.tensor.transpose(bank[:, a, u, :], blocks[first + a][:, u:WORDS:2], ident[:])
                banks.append(bank)
            grouped = ring.tile([P, len(blocks) * K_PASS], BF16, name="grouped", align_bytes=256)
            return banks, grouped

        def empty(copy, banks, grouped, i):
            words = grouped[:].bitcast(F32)[:, i * 2 * WORDS : (i + 1) * 2 * WORDS]
            copy(
                out=words.rearrange("p (a r u) -> p a r u", a=2, u=2),
                in_=banks[i][:].rearrange("p a u r -> p a r u"),
            )

        def quantise(codes, scales, values):
            nc.vector.quantize_mx(out=codes.bitcast(E5M2X4), scales=scales, in_=values)

        x_codes = keep.tile([P, TOKEN_TILES * PASSES * P], U32, align_bytes=256)
        x_scales = keep.tile([P, TOKEN_TILES * PASSES * P], U8, align_bytes=256)
        w_mx = {}

        def new_w_pair(g, pair):
            w_codes = ring.tile([P, 2 * N], U32, name="w_codes", bufs=4, align_bytes=256)
            w_scales = ring.tile([P, 2 * N], U8, name="w_scales", bufs=4, align_bytes=256)
            w_mx[(g, pair)] = (w_codes, w_scales)
            return w_codes, w_scales

        def quantise_x(grouped, j0, j1):
            cols = slice(j0 * PASSES * P, j1 * PASSES * P)
            quantise(x_codes[:, cols], x_scales[:, cols], grouped[:])

        tables = []

        def make_table(gain):
            table = keep.tile([P, TOKEN_TILES, 2, D], F32, name="table%d" % len(tables))
            nc.vector.tensor_tensor(
                out=table[:, :, 0, :], in0=cos_sb[:], in1=gain.to_broadcast([P, TOKEN_TILES, D]), op=ALU.mult
            )
            nc.vector.tensor_tensor(
                out=table[:, :, 1, :HALF],
                in0=sin_sb[:, :, HALF:],
                in1=gain[:, :, :HALF].to_broadcast([P, TOKEN_TILES, HALF]),
                op=ALU.mult,
            )
            nc.vector.scalar_tensor_tensor(
                out=table[:, :, 1, HALF:],
                in0=sin_sb[:, :, :HALF],
                scalar=-1.0,
                in1=gain[:, :, HALF:].to_broadcast([P, TOKEN_TILES, HALF]),
                op0=ALU.mult,
                op1=ALU.mult,
            )
            tables.append(table)

        def multiply(g, heads, tiles):
            acc = psum.tile([P, len(tiles), len(heads), D], F32, name="turned" if g == V_GROUP else "acc")
            for i, j in enumerate(tiles):
                for c in range(PASSES):
                    w_codes, w_scales = w_mx[(g, c // 2)]
                    x_cols = slice((j * PASSES + c) * P, (j * PASSES + c + 1) * P)
                    w_cols = slice((c % 2) * N + heads.start * D, (c % 2) * N + heads.stop * D)
                    nc.tensor.matmul_mx(
                        out=acc[:, i, :, :].rearrange("p h d -> p (h d)"),
                        lhsT=x_codes[:, x_cols].bitcast(E5M2X4),
                        lhsT_scale=x_scales[:, x_cols],
                        rhs=w_codes[:, w_cols].bitcast(E5M2X4),
                        rhs_scale=w_scales[:, w_cols],
                        start=(c == 0),
                        stop=(c == PASSES - 1),
                    )
            return acc

        waiting = []

        def sum_squares(acc):
            rows = acc[:].rearrange("p j h d -> p (j h) d")
            count = rows.shape[1]
            sums = ring.tile([P, count], F32, name="sums")
            squares = ring.tile([P, count, D], F32, name="squares", bufs=2)
            for r in range(count):
                nc.scalar.activation(
                    out=squares[:, r, :], in_=rows[:, r, :], func=ACT.Square, accum_out=sums[:, r : r + 1]
                )
                while waiting:
                    waiting.pop()()
            return sums

        def inverse_rms(sums):
            inv = ring.tile([P, sums.shape[1], 1], F32, name="inv")
            nc.scalar.activation(out=inv[:, :, 0], in_=sums[:], func=ACT.Abs_reciprocal_sqrt, scale=1.0 / D, bias=EPS)
            return inv

        def store(g, heads, tiles, result):
            dest = outs[g].rearrange("h (p j) d -> p h (j d)", j=TOKEN_TILES)
            nc.sync.dma_start(
                out=dest[:, heads.start : heads.stop, tiles.start * D : tiles.stop * D],
                in_=result[:].rearrange("p h j d -> p h (j d)"),
            )

        def new_result(heads, tiles):
            result = ring.tile([P, len(heads), len(tiles), D], F32, name="result", bufs=14)
            return result

        def products(g, heads, tiles, acc, inv):
            terms = ring.tile([P, len(heads), len(tiles), 2, D], F32, name="terms")
            for i, j in enumerate(tiles):
                for h in range(len(heads)):
                    nc.vector.scalar_tensor_tensor(
                        out=terms[:, h, i, :, :],
                        in0=acc[:, i, h : h + 1, :].to_broadcast([P, 2, D]),
                        scalar=inv[:, i * len(heads) + h, :],
                        in1=tables[g // K_GROUP][:, j, :, :],
                        op0=ALU.mult,
                        op1=ALU.mult,
                    )
            return terms

        def add_terms(engine, g, heads, tiles, terms):
            result = new_result(heads, tiles)
            halves = terms[:].rearrange("p h j s (t i) -> p (h j) s t i", t=2)
            engine.tensor_tensor(
                out=result[:].rearrange("p h j (t i) -> p (h j) t i", t=2),
                in0=halves[:, :, 0, :, :],
                in1=halves[:, :, 1, ::-1, :],
                op=ALU.add,
            )
            store(g, heads, tiles, result)

        def finish_rotary(piece, acc, sums):
            engine = nc.vector if piece == last_rotary else nc.gpsimd
            add_terms(engine, *piece, products(*piece, acc, inverse_rms(sums)))

        def finish_v(piece, acc, sums):
            g, heads, tiles = piece
            inv = inverse_rms(sums)
            result = new_result(heads, tiles)
            nc.vector.tensor_tensor(
                out=result[:].rearrange("p h j d -> p j h d"),
                in0=acc[:],
                in1=inv[:].rearrange("p (j h) o -> p j h o", h=len(heads)).to_broadcast([P, len(tiles), len(heads), D]),
                op=ALU.mult,
            )
            store(g, heads, tiles, result)

        for pair in range(2):
            new_w_pair(0, pair)
        for (kind, i), blocks in zip(head_order, head_runs):
            banks, grouped = transpose(blocks)
            empty(nc.vector.tensor_copy if kind == "x" else nc.scalar.copy, banks, grouped, 0)
            empty(nc.scalar.copy, banks, grouped, 1)
            if kind == "x":
                quantise_x(grouped, i, i + 1)
            else:
                for c in range(PASSES):
                    w_codes, w_scales = w_mx[(0, c // 2)]
                    cols = slice((c % 2) * N + i * D, (c % 2) * N + (i + 1) * D)
                    quantise(w_codes[:, cols], w_scales[:, cols], grouped[:, c * K_PASS : (c + 1) * K_PASS])
        gains = psum.tile([P, 2, D], F32, name="acc")
        nc.tensor.matmul(
            gains[:].rearrange("p t d -> p (t d)"),
            lhsT=ones[:],
            rhs=gain_rows[:].rearrange("p t d -> p (t d)"),
            start=True,
            stop=True,
        )
        for t in range(2):
            make_table(gains[:, t : t + 1, :])

        run_after = {0: "x", 1: (1, 0), 2: (1, 1)}
        for g in range(2, GROUPS):
            for pair in range(2):
                run_after[(g - 1) * TOKEN_TILES - 1 + 2 * pair] = (g, pair)

        pieces = [
            (g, range(h, h + 2), range(j, j + 2))
            for g in range(GROUPS)
            for j in range(0, TOKEN_TILES, 2)
            for h in range(0, HEADS, 2)
        ]
        last_rotary = pieces[V_GROUP * TOKEN_TILES - 1]
        g, heads, tiles = pieces.pop()
        pieces += [(g, heads, range(j, j + 1)) for j in tiles]

        for step, piece in enumerate(pieces):
            acc = multiply(*piece)
            sums = sum_squares(acc)
            run = run_after.get(step)
            if run is None:
                waiting.append(partial(finish_v if piece[0] == V_GROUP else finish_rotary, piece, acc, sums))
                continue
            banks, grouped = transpose(x_rest if run == "x" else w_runs[run])
            empty(nc.vector.tensor_copy, banks, grouped, 0)
            inv = inverse_rms(sums)
            for i in range(1, len(banks)):
                empty(nc.scalar.copy, banks, grouped, i)
            terms = products(*piece, acc, inv)
            if run == "x":
                quantise_x(grouped, 2, TOKEN_TILES)
            else:
                w_codes, w_scales = new_w_pair(*run)
                quantise(w_codes[:], w_scales[:], grouped[:])
            add_terms(nc.gpsimd, *piece, terms)
        waiting.pop()()
